import numpy as np
import ml_dtypes


def mxq(x, axis, fmt="e4m3"):
    dtype, down = {"e4m3": (ml_dtypes.float8_e4m3fn, 7), "e5m2": (ml_dtypes.float8_e5m2, 14)}[fmt]
    v = np.moveaxis(np.asarray(x, np.float32).astype(ml_dtypes.bfloat16).astype(np.float64), axis, -1)
    blocks = v.reshape(v.shape[:-1] + (-1, 32))
    amax = np.abs(blocks).max(-1, keepdims=True)
    byte = np.maximum(np.where(amax > 0, np.frexp(amax)[1] - 1 + 127, 0) - down, 1)
    scale = np.exp2(byte - 127.0)
    codes = (blocks / scale).astype(np.float32).astype(dtype).astype(np.float64)
    return np.moveaxis((codes * scale).reshape(v.shape), -1, axis)


WIDE = False


def mx_kscale(k):
    if not WIDE:
        return np.ones(k)
    levels = np.array([10, -10, 5, -5, 0])
    if k % 512:
        return np.exp2(np.random.permutation(np.resize(levels, k // 32))).repeat(32)
    a = np.empty((k // 512, 16))
    for p in range(k // 512):
        a[p, :8] = np.random.permutation(np.resize(levels, 8))
        for g in range(8):
            far = levels[np.abs(levels - a[p, g]) >= 10]
            a[p, g + 8] = far[np.random.randint(len(far))]
    return np.exp2(a.ravel()).repeat(32)


BF16 = ml_dtypes.bfloat16


def bf(x):
    return np.asarray(x, np.float32).astype(BF16)


def f64(x):
    return np.asarray(x).astype(np.float64)


B, N, D = 1, 1024, 1024
P0 = 0.2


def setup_inputs():
    s = mx_kscale(D)
    g = 0.4 + 1.2 * np.random.random_sample((B, 1, N))
    bound = np.sqrt(6.0 / (D + D))
    return {"embedding": bf(np.random.standard_normal((B, D, N)) * g * np.sqrt(P0) / D ** 0.25 * s[None, :, None]),
            "heatm": bf(np.random.standard_normal((B, D, N))),
            "W_b": bf(np.random.uniform(-bound, bound, (D, D)) / s[:, None] / s[None, :])}


def reference(embedding, heatm, W_b):
    eq = mxq(f64(embedding), 1, "e4m3")
    t = np.swapaxes(eq, 1, 2) @ mxq(f64(W_b), 0, "e4m3")
    C = np.tanh(mxq(t, 2, "e4m3") @ eq)
    max_cow = np.max(C, axis=-1, keepdims=True)
    e = np.exp(max_cow - np.max(max_cow, axis=1, keepdims=True))
    return e / np.sum(e, axis=1, keepdims=True)

@@ -1,0 +1,213 @@
+from contextlib import ExitStack
+
+import concourse.mybir as mybir
+from concourse.masks import make_identity
+
+FLOPS = 2 * 2 * 1024 * 1024 * 1024
+BYTES = 2 * 1024 * 1024 * 2 + 1024 * 4
+
+F32 = mybir.dt.float32
+BF16 = mybir.dt.bfloat16
+U32 = mybir.dt.uint32
+U8 = mybir.dt.uint8
+FP8X4 = mybir.dt.float8_e4m3fn_x4
+ACT = mybir.ActivationFunctionType
+ALU = mybir.AluOpType
+AX = mybir.AxisListType
+
+P = 128
+PACK = 4
+G = 2
+HCOL = 512
+NB = 8
+
+SCHEDULE = [
+    ("ld", "e", 0, 0), ("ld", "e", 0, 1), ("ld", "w", 0, 0), ("ld", "w", 0, 1),
+    ("ld", "w", 1, 0), ("ld", "w", 1, 1), ("ld", "e", 1, 0), ("ld", "e", 1, 1),
+    ("wu", "e", 0, 1, 4), ("wu", "w", 0, 0, 4), ("wu", "w", 0, 1, 2), ("rg", "e", 0, 0, 2, "v"),
+    ("rg", "e", 0, 2, 2, "s"), ("qz", "e", 0, 0, 2), ("rg", "e", 1, 0, 2, "v"), ("rg", "e", 1, 2, 2, "s"),
+    ("qz", "e", 0, 2, 2), ("qz", "e", 1, 0, 2), ("rg", "w", 0, 0, 2, "v"), ("rg", "w", 0, 2, 2, "s"),
+    ("qz", "e", 1, 2, 2), ("qz", "w", 0, 0, 2), ("rg", "w", 1, 0, 1, "v"), ("rg", "w", 1, 2, 1, "s"),
+    ("rg", "w", 1, 1, 1, "v"), ("rg", "w", 1, 3, 1, "s"), ("qz", "w", 1, 0, 1), ("qz", "w", 0, 2, 2),
+    ("cell", 0, 0, 1), ("qz", "w", 1, 2, 1), ("cell", 0, 0, 3), ("qz", "w", 1, 1, 1),
+    ("rg", "w", 0, 6, 2, "s"), ("cell", 0, 0, 2), ("rg", "w", 0, 4, 2, "v"), ("cell", 0, 2, 3),
+    ("cell", 0, 1, 1), ("cell", 0, 1, 2), ("cell", 0, 2, 0), ("qz", "w", 1, 3, 1),
+    ("cell", 0, 2, 1), ("qz", "w", 0, 4, 2), ("cell", 0, 2, 2), ("cell", 0, 3, 3),
+    ("rg", "w", 1, 4, 1, "v"), ("rg", "w", 1, 6, 1, "s"), ("cell", 0, 3, 2), ("cell", 0, 3, 1),
+    ("rg", "w", 1, 5, 1, "v"), ("cell", 0, 0, 0), ("cell", 0, 3, 0), ("rg", "w", 1, 7, 1, "s"),
+    ("qz", "w", 1, 4, 1), ("cell", 0, 1, 0), ("qz", "w", 0, 6, 2), ("cell", 0, 1, 3),
+    ("cell", 1, 0, 0), ("qz", "w", 1, 5, 1), ("co", 0, 2), ("cell", 1, 0, 2),
+    ("rg", "e", 0, 4, 2, "v"), ("cell", 1, 1, 0), ("cell", 1, 0, 1), ("co", 0, 1),
+    ("cell", 1, 1, 2), ("qz", "w", 1, 6, 1), ("cell", 1, 0, 3), ("qz", "w", 1, 7, 1),
+    ("cell", 1, 1, 1), ("qz", "e", 0, 4, 2), ("cell", 1, 2, 0), ("co", 0, 3),
+    ("cell", 1, 3, 3), ("rg", "e", 1, 4, 2, "v"), ("cell", 1, 3, 1), ("cell", 1, 2, 1),
+    ("cell", 1, 2, 2), ("co", 0, 0), ("cell", 1, 3, 2), ("qz", "e", 1, 4, 2),
+    ("cell", 1, 3, 0), ("cell", 1, 2, 3), ("co", 1, 2), ("rg", "e", 0, 6, 2, "v"),
+    ("cell", 1, 1, 3), ("cell", 1, 2, 4), ("cell", 1, 3, 5), ("cell", 0, 2, 5),
+    ("co", 1, 0), ("rg", "e", 1, 6, 2, "v"), ("cell", 1, 0, 4), ("cell", 0, 3, 5),
+    ("cell", 1, 2, 5), ("co", 1, 1), ("cell", 0, 2, 4), ("qt", 2),
+    ("cell", 1, 1, 4), ("qz", "e", 0, 6, 2), ("cell", 1, 1, 5), ("cell", 1, 0, 5),
+    ("qz", "e", 1, 6, 2), ("cell", 0, 0, 5), ("cell", 1, 3, 4), ("co", 1, 5),
+    ("qt", 1), ("cell", 0, 1, 5), ("m2", 2, 0), ("co", 1, 3),
+    ("cell", 1, 0, 6), ("cell", 0, 1, 4), ("cell", 0, 0, 4), ("co", 1, 4),
+    ("qt", 3), ("cell", 0, 3, 4), ("m2", 1, 1), ("qt", 0),
+    ("co", 0, 5), ("rm", 2, 0), ("m2", 1, 0), ("co", 0, 4),
+    ("qt", 5), ("m2", 3, 0), ("rm", 1, 1), ("cell", 1, 2, 6),
+    ("cell", 1, 1, 6), ("rm", 3, 0), ("cell", 0, 1, 6), ("cell", 1, 3, 6),
+    ("cell", 0, 3, 6), ("m2", 5, 0), ("co", 1, 6), ("rm", 1, 0),
+    ("m2", 0, 0), ("qt", 4), ("cell", 1, 1, 7), ("cell", 0, 0, 6),
+    ("rm", 0, 0), ("cell", 0, 2, 6), ("m2", 3, 1), ("co", 0, 6),
+    ("rm", 5, 0), ("cell", 0, 1, 7), ("m2", 0, 1), ("qt", 6),
+    ("cell", 0, 3, 7), ("rm", 3, 1), ("m2", 4, 1), ("rm", 0, 1),
+    ("cell", 1, 0, 7), ("cell", 0, 2, 7), ("cell", 1, 3, 7), ("m2", 4, 0),
+    ("rm", 4, 1), ("cell", 1, 2, 7), ("m2", 2, 1), ("rm", 4, 0),
+    ("co", 1, 7), ("cell", 0, 0, 7), ("m2", 5, 1), ("rm", 2, 1),
+    ("co", 0, 7), ("m2", 6, 0), ("rm", 5, 1), ("m2", 6, 1),
+    ("qt", 7), ("rm", 6, 0), ("m2", 7, 1), ("rm", 6, 1),
+    ("m2", 7, 0), ("rm", 7, 1), ("rm", 7, 0),
+]
+
+
+def tile_parallelcoattention_kernel(tc, embedding, heatm, W_b, out):
+    nc = tc.nc
+    e_rows = embedding[0].rearrange("(g p t) n -> p g t n", p=P, t=PACK)
+    w_rows = W_b.rearrange("(g p t) n -> p g t n", p=P, t=PACK)
+    out_rows = out[0].rearrange("(c q) u -> c (q u)", c=NB)
+
+    with ExitStack() as ctx:
+        keep = ctx.enter_context(tc.tile_pool(name="keep", bufs=1))
+        psum = ctx.enter_context(tc.psum_pool(name="psum", bufs=8))
+        ctx.enter_context(tc.manual_schedule())
+
+        warm = keep.tile([P, 1], F32, name="warm")
+        nc.vector.memset(warm[:], 0.0)
+        warm2 = keep.tile([P, 1], F32, name="warm2")
+        nc.scalar.activation(out=warm2[:], in_=warm[:], func=ACT.Tanh)
+        ident = keep.tile([P, P], F32, name="ident")
+        make_identity(nc, ident[:])
+        ones = keep.tile([P, P], F32, name="ones")
+        nc.vector.memset(ones[:], 1.0)
+        epad = keep.tile([P, P], F32, name="epad")
+        nc.vector.memset(epad[:], 0.0)
+        shift = keep.tile([P, 1], F32, name="shift")
+        nc.vector.memset(shift[:], -1.0)
+        mx16 = keep.tile([P, 2 * NB], F32, name="mx16")
+
+        raw = {}
+        grp = {}
+        cod = {}
+        scl = {}
+        for kind in ("e", "w"):
+            for h in range(2):
+                key = (kind, h)
+                grp[key] = keep.tile([P, G, HCOL, PACK], BF16, name="grp_%s%d" % key, align_bytes=64)
+                cod[key] = keep.tile([P, G, HCOL], U32, name="cod_%s%d" % key, align_bytes=64)
+                scl[key] = keep.tile([P, G, HCOL], U8, name="scl_%s%d" % key, align_bytes=64)
+        tgr = {}
+        tcod = {}
+        tscl = {}
+        for b in range(NB):
+            tgr[b] = keep.tile([P, G, P, PACK], BF16, name="tgr%d" % b, align_bytes=64)
+            tcod[b] = keep.tile([P, G, P], U32, name="tcod%d" % b, align_bytes=64)
+            tscl[b] = keep.tile([P, G, P], U8, name="tscl%d" % b, align_bytes=64)
+        pts = {}
+        pcs = {}
+
+        def cols(c0, nchunk):
+            return slice((c0 % 4) * P, (c0 % 4 + nchunk) * P)
+
+        def load(kind, h, g):
+            rows = e_rows if kind == "e" else w_rows
+            raw[(kind, h, g)] = keep.tile([P, PACK, HCOL], BF16, name="raw_%s%d%d" % (kind, h, g))
+            nc.sync.dma_start(out=raw[(kind, h, g)][:],
+                              in_=rows[:, g, :, h * HCOL:(h + 1) * HCOL])
+
+        def regroup(kind, g, c0, nchunk, eng):
+            if kind == "e":
+                src = raw[(kind, c0 // 4, g)][:, :, cols(c0, nchunk)].rearrange("p t (c i) -> p c t i", i=4)
+                dst = grp[(kind, c0 // 4)][:, g, cols(c0, nchunk), :].rearrange("p (c i) t -> p c t i", i=4)
+            else:
+                j0 = c0 % 4
+                src = raw[(kind, c0 // 4, g)][:].rearrange("p t (m j) -> p j m t", j=4)[:, j0:j0 + nchunk]
+                dst = grp[(kind, c0 // 4)][:, g, cols(c0, nchunk), :].rearrange("p (j m) t -> p j m t", m=P)
+            if eng == "v":
+                nc.vector.tensor_copy(out=dst, in_=src)
+            else:
+                nc.scalar.copy(out=dst, in_=src)
+
+        def quantise(kind, g, c0, nchunk):
+            key = (kind, c0 // 4)
+            nc.vector.quantize_mx(
+                out=cod[key][:, g, cols(c0, nchunk)].bitcast(FP8X4),
+                scales=scl[key][:, g, cols(c0, nchunk)],
+                in_=grp[key][:, g, cols(c0, nchunk), :].rearrange("p n t -> p (n t)"),
+            )
+
+        def cell(g2, j, b):
+            if (g2, b) not in pts:
+                pts[(g2, b)] = psum.tile([P, PACK, P], F32, name="pt", tag="bank")
+            for g1 in range(G):
+                nc.tensor.matmul_mx(
+                    out=pts[(g2, b)][:, j, :],
+                    lhsT=cod[("w", g2)][:, g1, cols(j, 1)].bitcast(FP8X4),
+                    lhsT_scale=scl[("w", g2)][:, g1, cols(j, 1)],
+                    rhs=cod[("e", b // 4)][:, g1, cols(b, 1)].bitcast(FP8X4),
+                    rhs_scale=scl[("e", b // 4)][:, g1, cols(b, 1)],
+                    start=(g1 == 0),
+                    stop=(g1 == G - 1),
+                )
+
+        def copy_out(g2, b):
+            nc.scalar.copy(out=tgr[b][:, g2], in_=pts[(g2, b)][:].rearrange("p j n -> p n j"))
+
+        def quantise_t(b):
+            nc.vector.quantize_mx(
+                out=tcod[b][:].rearrange("p g n -> p (g n)").bitcast(FP8X4),
+                scales=tscl[b][:].rearrange("p g n -> p (g n)"),
+                in_=tgr[b][:].rearrange("p g n t -> p (g n t)"),
+            )
+
+        def mm2(b, h):
+            pc = psum.tile([P, HCOL], F32, name="pc", tag="bank")
+            pcs[(b, h)] = pc
+            for g2 in range(G):
+                nc.tensor.matmul_mx(
+                    out=pc[:],
+                    lhsT=tcod[b][:, g2, :].bitcast(FP8X4),
+                    lhsT_scale=tscl[b][:, g2, :],
+                    rhs=cod[("e", h)][:, g2, :].bitcast(FP8X4),
+                    rhs_scale=scl[("e", h)][:, g2, :],
+                    start=(g2 == 0),
+                    stop=(g2 == G - 1),
+                )
+
+        def row_max(b, h):
+            nc.vector.reduce_max(out=mx16[:, 2 * b + h:2 * b + h + 1], in_=pcs[(b, h)][:], axis=AX.X)
+
+        def warm_up(kind, h, g, count):
+            junk = psum.tile([P, HCOL], F32, name="junk", tag="bank")
+            for i in range(count):
+                nc.tensor.matmul(out=junk[:], lhsT=raw[(kind, h, g)][:, 0, 0:P], rhs=raw[(kind, h, g)][:, 1, :],
+                                 start=True, stop=True)
+
+        steps = {"wu": warm_up, "ld": load, "rg": regroup, "qz": quantise, "cell": cell, "co": copy_out,
+                 "qt": quantise_t, "m2": mm2, "rm": row_max}
+        for step in SCHEDULE:
+            steps[step[0]](*step[1:])
+
+        m8 = keep.tile([P, NB], F32, name="m8")
+        nc.vector.reduce_max(out=m8[:], in_=mx16[:].rearrange("p (b h) -> p b h", h=2), axis=AX.X)
+        th = keep.tile([P, NB], F32, name="th")
+        nc.scalar.activation(out=th[:], in_=m8[:], func=ACT.Tanh)
+        rsum = keep.tile([P, 1], F32, name="rsum")
+        nc.scalar.activation(out=epad[:, 0:NB], in_=th[:], func=ACT.Exp, bias=shift[:, 0:1], scale=1.0,
+                             accum_out=rsum[:])
+        et = psum.tile([P, P], F32, name="et", tag="bank")
+        nc.tensor.transpose(et[:], epad[:], ident[:])
+        tot = psum.tile([P, 1], F32, name="tot", tag="bank")
+        nc.tensor.matmul(out=tot[:], lhsT=ones[:], rhs=rsum[:], start=True, stop=True)
+        rc = keep.tile([P, 1], F32, name="rc")
+        nc.vector.reciprocal(out=rc[:], in_=tot[:])
+        res = keep.tile([P, P], F32, name="res")
+        nc.vector.tensor_scalar(out=res[:], in0=et[:], scalar1=rc[:, 0:1], scalar2=None, op0=ALU.mult)
+        nc.sync.dma_start(out=out_rows, in_=res[0:NB, :])

@@ -21,52 +21,6 @@ G = 2
 HCOL = 512
 NB = 8
 
-SCHEDULE = [
-    ("ld", "e", 0, 0), ("ld", "e", 0, 1), ("ld", "w", 0, 0), ("ld", "w", 0, 1),
-    ("ld", "w", 1, 0), ("ld", "w", 1, 1), ("ld", "e", 1, 0), ("ld", "e", 1, 1),
-    ("wu", "e", 0, 1, 4), ("wu", "w", 0, 0, 4), ("wu", "w", 0, 1, 2), ("rg", "e", 0, 0, 2, "v"),
-    ("rg", "e", 0, 2, 2, "s"), ("qz", "e", 0, 0, 2), ("rg", "e", 1, 0, 2, "v"), ("rg", "e", 1, 2, 2, "s"),
-    ("qz", "e", 0, 2, 2), ("qz", "e", 1, 0, 2), ("rg", "w", 0, 0, 2, "v"), ("rg", "w", 0, 2, 2, "s"),
-    ("qz", "e", 1, 2, 2), ("qz", "w", 0, 0, 2), ("rg", "w", 1, 0, 1, "v"), ("rg", "w", 1, 2, 1, "s"),
-    ("rg", "w", 1, 1, 1, "v"), ("rg", "w", 1, 3, 1, "s"), ("qz", "w", 1, 0, 1), ("qz", "w", 0, 2, 2),
-    ("cell", 0, 0, 1), ("qz", "w", 1, 2, 1), ("cell", 0, 0, 3), ("qz", "w", 1, 1, 1),
-    ("rg", "w", 0, 6, 2, "s"), ("cell", 0, 0, 2), ("rg", "w", 0, 4, 2, "v"), ("cell", 0, 2, 3),
-    ("cell", 0, 1, 1), ("cell", 0, 1, 2), ("cell", 0, 2, 0), ("qz", "w", 1, 3, 1),
-    ("cell", 0, 2, 1), ("qz", "w", 0, 4, 2), ("cell", 0, 2, 2), ("cell", 0, 3, 3),
-    ("rg", "w", 1, 4, 1, "v"), ("rg", "w", 1, 6, 1, "s"), ("cell", 0, 3, 2), ("cell", 0, 3, 1),
-    ("rg", "w", 1, 5, 1, "v"), ("cell", 0, 0, 0), ("cell", 0, 3, 0), ("rg", "w", 1, 7, 1, "s"),
-    ("qz", "w", 1, 4, 1), ("cell", 0, 1, 0), ("qz", "w", 0, 6, 2), ("cell", 0, 1, 3),
-    ("cell", 1, 0, 0), ("qz", "w", 1, 5, 1), ("co", 0, 2), ("cell", 1, 0, 2),
-    ("rg", "e", 0, 4, 2, "v"), ("cell", 1, 1, 0), ("cell", 1, 0, 1), ("co", 0, 1),
-    ("cell", 1, 1, 2), ("qz", "w", 1, 6, 1), ("cell", 1, 0, 3), ("qz", "w", 1, 7, 1),
-    ("cell", 1, 1, 1), ("qz", "e", 0, 4, 2), ("cell", 1, 2, 0), ("co", 0, 3),
-    ("cell", 1, 3, 3), ("rg", "e", 1, 4, 2, "v"), ("cell", 1, 3, 1), ("cell", 1, 2, 1),
-    ("cell", 1, 2, 2), ("co", 0, 0), ("cell", 1, 3, 2), ("qz", "e", 1, 4, 2),
-    ("cell", 1, 3, 0), ("cell", 1, 2, 3), ("co", 1, 2), ("rg", "e", 0, 6, 2, "v"),
-    ("cell", 1, 1, 3), ("cell", 1, 2, 4), ("cell", 1, 3, 5), ("cell", 0, 2, 5),
-    ("co", 1, 0), ("rg", "e", 1, 6, 2, "v"), ("cell", 1, 0, 4), ("cell", 0, 3, 5),
-    ("cell", 1, 2, 5), ("co", 1, 1), ("cell", 0, 2, 4), ("qt", 2),
-    ("cell", 1, 1, 4), ("qz", "e", 0, 6, 2), ("cell", 1, 1, 5), ("cell", 1, 0, 5),
-    ("qz", "e", 1, 6, 2), ("cell", 0, 0, 5), ("cell", 1, 3, 4), ("co", 1, 5),
-    ("qt", 1), ("cell", 0, 1, 5), ("m2", 2, 0), ("co", 1, 3),
-    ("cell", 1, 0, 6), ("cell", 0, 1, 4), ("cell", 0, 0, 4), ("co", 1, 4),
-    ("qt", 3), ("cell", 0, 3, 4), ("m2", 1, 1), ("qt", 0),
-    ("co", 0, 5), ("rm", 2, 0), ("m2", 1, 0), ("co", 0, 4),
-    ("qt", 5), ("m2", 3, 0), ("rm", 1, 1), ("cell", 1, 2, 6),
-    ("cell", 1, 1, 6), ("rm", 3, 0), ("cell", 0, 1, 6), ("cell", 1, 3, 6),
-    ("cell", 0, 3, 6), ("m2", 5, 0), ("co", 1, 6), ("rm", 1, 0),
-    ("m2", 0, 0), ("qt", 4), ("cell", 1, 1, 7), ("cell", 0, 0, 6),
-    ("rm", 0, 0), ("cell", 0, 2, 6), ("m2", 3, 1), ("co", 0, 6),
-    ("rm", 5, 0), ("cell", 0, 1, 7), ("m2", 0, 1), ("qt", 6),
-    ("cell", 0, 3, 7), ("rm", 3, 1), ("m2", 4, 1), ("rm", 0, 1),
-    ("cell", 1, 0, 7), ("cell", 0, 2, 7), ("cell", 1, 3, 7), ("m2", 4, 0),
-    ("rm", 4, 1), ("cell", 1, 2, 7), ("m2", 2, 1), ("rm", 4, 0),
-    ("co", 1, 7), ("cell", 0, 0, 7), ("m2", 5, 1), ("rm", 2, 1),
-    ("co", 0, 7), ("m2", 6, 0), ("rm", 5, 1), ("m2", 6, 1),
-    ("qt", 7), ("rm", 6, 0), ("m2", 7, 1), ("rm", 6, 1),
-    ("m2", 7, 0), ("rm", 7, 1), ("rm", 7, 0),
-]
-
 
 def tile_parallelcoattention_kernel(tc, embedding, heatm, W_b, out):
     nc = tc.nc
@@ -103,6 +57,8 @@ def tile_parallelcoattention_kernel(tc, embedding, heatm, W_b, out):
                 grp[key] = keep.tile([P, G, HCOL, PACK], BF16, name="grp_%s%d" % key, align_bytes=64)
                 cod[key] = keep.tile([P, G, HCOL], U32, name="cod_%s%d" % key, align_bytes=64)
                 scl[key] = keep.tile([P, G, HCOL], U8, name="scl_%s%d" % key, align_bytes=64)
+                for g in range(G):
+                    raw[(kind, g, h)] = keep.tile([P, PACK, HCOL], BF16, name="raw_%s%d%d" % (kind, g, h))
         tgr = {}
         tcod = {}
         tscl = {}
@@ -113,54 +69,53 @@ def tile_parallelcoattention_kernel(tc, embedding, heatm, W_b, out):
         pts = {}
         pcs = {}
 
-        def cols(c0, nchunk):
-            return slice((c0 % 4) * P, (c0 % 4 + nchunk) * P)
+        def cols(c0, n):
+            return slice(c0 * P, (c0 + n) * P)
 
-        def load(kind, h, g):
+        def load(kind, g, h, c0=0, n=4):
             rows = e_rows if kind == "e" else w_rows
-            raw[(kind, h, g)] = keep.tile([P, PACK, HCOL], BF16, name="raw_%s%d%d" % (kind, h, g))
-            nc.sync.dma_start(out=raw[(kind, h, g)][:],
-                              in_=rows[:, g, :, h * HCOL:(h + 1) * HCOL])
+            nc.sync.dma_start(out=raw[(kind, g, h)][:, :, cols(c0, n)],
+                              in_=rows[:, g, :, h * HCOL + c0 * P:h * HCOL + (c0 + n) * P])
 
-        def regroup(kind, g, c0, nchunk, eng):
+        def copy(kind, g, h, c0, n, eng):
             if kind == "e":
-                src = raw[(kind, c0 // 4, g)][:, :, cols(c0, nchunk)].rearrange("p t (c i) -> p c t i", i=4)
-                dst = grp[(kind, c0 // 4)][:, g, cols(c0, nchunk), :].rearrange("p (c i) t -> p c t i", i=4)
+                src = raw[(kind, g, h)][:, :, cols(c0, n)].rearrange("p t (c i) -> p c t i", i=4)
+                dst = grp[(kind, h)][:, g, cols(c0, n), :].rearrange("p (c i) t -> p c t i", i=4)
             else:
-                j0 = c0 % 4
-                src = raw[(kind, c0 // 4, g)][:].rearrange("p t (m j) -> p j m t", j=4)[:, j0:j0 + nchunk]
-                dst = grp[(kind, c0 // 4)][:, g, cols(c0, nchunk), :].rearrange("p (j m) t -> p j m t", m=P)
+                src = raw[(kind, g, h)][:, :, cols(c0, n)].rearrange("p t (m j) -> p m t j", j=4)
+                dst = grp[(kind, h)][:, g].rearrange("p (j m) t -> p m t j", j=4)[:, c0 * 32:(c0 + n) * 32]
             if eng == "v":
                 nc.vector.tensor_copy(out=dst, in_=src)
             else:
                 nc.scalar.copy(out=dst, in_=src)
 
-        def quantise(kind, g, c0, nchunk):
-            key = (kind, c0 // 4)
+        def quant(kind, g, h, c0, n):
+            key = (kind, h)
             nc.vector.quantize_mx(
-                out=cod[key][:, g, cols(c0, nchunk)].bitcast(FP8X4),
-                scales=scl[key][:, g, cols(c0, nchunk)],
-                in_=grp[key][:, g, cols(c0, nchunk), :].rearrange("p n t -> p (n t)"),
+                out=cod[key][:, g, cols(c0, n)].bitcast(FP8X4),
+                scales=scl[key][:, g, cols(c0, n)],
+                in_=grp[key][:, g, cols(c0, n), :].rearrange("p n t -> p (n t)"),
             )
 
-        def cell(g2, j, b):
+        def cells(g2, b, js=range(4)):
             if (g2, b) not in pts:
                 pts[(g2, b)] = psum.tile([P, PACK, P], F32, name="pt", tag="bank")
-            for g1 in range(G):
-                nc.tensor.matmul_mx(
-                    out=pts[(g2, b)][:, j, :],
-                    lhsT=cod[("w", g2)][:, g1, cols(j, 1)].bitcast(FP8X4),
-                    lhsT_scale=scl[("w", g2)][:, g1, cols(j, 1)],
-                    rhs=cod[("e", b // 4)][:, g1, cols(b, 1)].bitcast(FP8X4),
-                    rhs_scale=scl[("e", b // 4)][:, g1, cols(b, 1)],
-                    start=(g1 == 0),
-                    stop=(g1 == G - 1),
-                )
+            for j in js:
+                for g1 in range(G):
+                    nc.tensor.matmul_mx(
+                        out=pts[(g2, b)][:, j, :],
+                        lhsT=cod[("w", g2)][:, g1, cols(j, 1)].bitcast(FP8X4),
+                        lhsT_scale=scl[("w", g2)][:, g1, cols(j, 1)],
+                        rhs=cod[("e", b // 4)][:, g1, cols(b % 4, 1)].bitcast(FP8X4),
+                        rhs_scale=scl[("e", b // 4)][:, g1, cols(b % 4, 1)],
+                        start=(g1 == 0),
+                        stop=(g1 == G - 1),
+                    )
 
-        def copy_out(g2, b):
+        def copy_t(g2, b):
             nc.scalar.copy(out=tgr[b][:, g2], in_=pts[(g2, b)][:].rearrange("p j n -> p n j"))
 
-        def quantise_t(b):
+        def quant_t(b):
             nc.vector.quantize_mx(
                 out=tcod[b][:].rearrange("p g n -> p (g n)").bitcast(FP8X4),
                 scales=tscl[b][:].rearrange("p g n -> p (g n)"),
@@ -184,28 +139,119 @@ def tile_parallelcoattention_kernel(tc, embedding, heatm, W_b, out):
         def row_max(b, h):
             nc.vector.reduce_max(out=mx16[:, 2 * b + h:2 * b + h + 1], in_=pcs[(b, h)][:], axis=AX.X)
 
-        def warm_up(kind, h, g, count):
+        def warm_up(kind, g, h, count):
             junk = psum.tile([P, HCOL], F32, name="junk", tag="bank")
             for i in range(count):
-                nc.tensor.matmul(out=junk[:], lhsT=raw[(kind, h, g)][:, 0, 0:P], rhs=raw[(kind, h, g)][:, 1, :],
+                nc.tensor.matmul(out=junk[:], lhsT=raw[(kind, g, h)][:, 0, 0:P], rhs=raw[(kind, g, h)][:, 1, :],
                                  start=True, stop=True)
 
-        steps = {"wu": warm_up, "ld": load, "rg": regroup, "qz": quantise, "cell": cell, "co": copy_out,
-                 "qt": quantise_t, "m2": mm2, "rm": row_max}
-        for step in SCHEDULE:
-            steps[step[0]](*step[1:])
-
+        e0, w0, w1, e1 = ("e", 0, 0), ("w", 0, 0), ("w", 1, 0), ("e", 1, 0)
+        x0, x1, f0, f1 = ("w", 0, 1), ("w", 1, 1), ("e", 0, 1), ("e", 1, 1)
+        load(*e0, 0, 2)
+        load(*e0, 2, 2)
+        load(*w0)
+        load(*w1)
+        load(*e1, 0, 2)
+        load(*e1, 2, 2)
+        for p in (x0, x1, f0, f1):
+            load(*p)
+        warm_up("e", 0, 0, 4)
+        warm_up("w", 0, 0, 4)
+        warm_up("w", 1, 0, 2)
+        copy(*e0, 0, 1, "v")
+        copy(*e0, 1, 1, "s")
+        copy(*e0, 2, 1, "v")
+        copy(*e0, 3, 1, "s")
+        quant(*e0, 0, 2)
+        copy(*w0, 0, 2, "v")
+        copy(*w0, 2, 2, "s")
+        quant(*e0, 2, 2)
+        copy(*w1, 0, 2, "v")
+        copy(*w1, 2, 2, "s")
+        quant(*w0, 0, 4)
+        copy(*e1, 0, 1, "v")
+        copy(*e1, 1, 1, "s")
+        quant(*w1, 0, 4)
+        quant(*e1, 0, 1)
+        quant(*e1, 1, 1)
+        copy(*e1, 2, 1, "v")
+        copy(*e1, 3, 1, "s")
+        cells(0, 0)
+        cells(0, 1)
+        copy(*x0, 0, 2, "v")
+        quant(*e1, 2, 2)
+        copy(*x0, 2, 2, "s")
+        cells(0, 2)
+        cells(0, 3)
+        copy(*x1, 0, 2, "v")
+        copy(*x1, 2, 2, "s")
+        quant(*x0, 0, 4)
+        quant(*x1, 0, 2)
+        quant(*x1, 2, 2)
+        for b in range(4):
+            copy_t(0, b)
+        for b in range(4):
+            cells(1, b)
+        copy(*f0, 0, 2, "v")
+        copy(*f1, 0, 2, "v")
+        for b in range(4):
+            copy_t(1, b)
+        quant(*f0, 0, 2)
+        quant(*f1, 0, 2)
+        quant_t(0)
+        quant_t(1)
+        cells(0, 4)
+        cells(1, 4)
+        mm2(0, 0)
+        mm2(1, 0)
+        for p in (f0, f1):
+            copy(*p, 3, 1, "s")
+            copy(*p, 2, 1, "v")
+        copy_t(0, 4)
+        copy_t(1, 4)
+        quant_t(2)
+        quant_t(3)
+        mm2(2, 0)
+        mm2(3, 0)
+        row_max(0, 0)
+        row_max(1, 0)
+        quant(*f0, 2, 2)
+        quant(*f1, 2, 2)
+        row_max(2, 0)
+        quant_t(4)
+        row_max(3, 0)
+        for b in range(5, NB):
+            cells(0, b)
+            copy_t(0, b)
+            mm2(b - 5, 1)
+            cells(1, b)
+            copy_t(1, b)
+            row_max(b - 5, 1)
+            mm2(b - 1, 0)
+            mm2(b - 1, 1)
+            row_max(b - 1, 0)
+            quant_t(b)
+            row_max(b - 1, 1)
+        mm2(3, 1)
+        row_max(3, 1)
+        mm2(7, 0)
+        mm2(7, 1)
+        row_max(7, 0)
         m8 = keep.tile([P, NB], F32, name="m8")
-        nc.vector.reduce_max(out=m8[:], in_=mx16[:].rearrange("p (b h) -> p b h", h=2), axis=AX.X)
+        nc.vector.reduce_max(out=m8[:, 0:NB - 1], in_=mx16[:, 0:2 * NB - 2].rearrange("p (b h) -> p b h", h=2), axis=AX.X)
+        junk_max = keep.tile([P, HCOL], F32, name="junk_max")
+        nc.vector.tensor_scalar(out=junk_max[:], in0=pcs[(7, 1)][:], scalar1=0.0, scalar2=mx16[:, 14:15], op0=ALU.add,
+                                op1=ALU.max, accum_out=m8[:, NB - 1:NB])
+
         th = keep.tile([P, NB], F32, name="th")
         nc.scalar.activation(out=th[:], in_=m8[:], func=ACT.Tanh)
         rsum = keep.tile([P, 1], F32, name="rsum")
         nc.scalar.activation(out=epad[:, 0:NB], in_=th[:], func=ACT.Exp, bias=shift[:, 0:1], scale=1.0,
                              accum_out=rsum[:])
-        et = psum.tile([P, P], F32, name="et", tag="bank")
-        nc.tensor.transpose(et[:], epad[:], ident[:])
         tot = psum.tile([P, 1], F32, name="tot", tag="bank")
         nc.tensor.matmul(out=tot[:], lhsT=ones[:], rhs=rsum[:], start=True, stop=True)
+        et = psum.tile([P, P], F32, name="et", tag="bank")
+        nc.tensor.transpose(et[:], epad[:], ident[:])
         rc = keep.tile([P, 1], F32, name="rc")
         nc.vector.reciprocal(out=rc[:], in_=tot[:])
         res = keep.tile([P, P], F32, name="res")

@@ -147,12 +147,10 @@ def tile_parallelcoattention_kernel(tc, embedding, heatm, W_b, out):
 
         e0, w0, w1, e1 = ("e", 0, 0), ("w", 0, 0), ("w", 1, 0), ("e", 1, 0)
         x0, x1, f0, f1 = ("w", 0, 1), ("w", 1, 1), ("e", 0, 1), ("e", 1, 1)
-        load(*e0, 0, 2)
-        load(*e0, 2, 2)
+        load(*e0)
         load(*w0)
         load(*w1)
-        load(*e1, 0, 2)
-        load(*e1, 2, 2)
+        load(*e1)
         for p in (x0, x1, f0, f1):
             load(*p)
         warm_up("e", 0, 0, 4)

@@ -82,8 +82,8 @@ def tile_parallelcoattention_kernel(tc, embedding, heatm, W_b, out):
                 src = raw[(kind, g, h)][:, :, cols(c0, n)].rearrange("p t (c i) -> p c t i", i=4)
                 dst = grp[(kind, h)][:, g, cols(c0, n), :].rearrange("p (c i) t -> p c t i", i=4)
             else:
-                src = raw[(kind, g, h)][:, :, cols(c0, n)].rearrange("p t (m j) -> p m t j", j=4)
-                dst = grp[(kind, h)][:, g].rearrange("p (j m) t -> p m t j", j=4)[:, c0 * 32:(c0 + n) * 32]
+                src = raw[(kind, g, h)][:].rearrange("p t (m u j) -> p j m t u", u=2, j=4)[:, c0:c0 + n]
+                dst = grp[(kind, h)][:, g, cols(c0, n), :].rearrange("p (j m u) t -> p j m t u", u=2, m=P // 2)
             if eng == "v":
                 nc.vector.tensor_copy(out=dst, in_=src)
             else:
@@ -147,53 +147,51 @@ def tile_parallelcoattention_kernel(tc, embedding, heatm, W_b, out):
 
         e0, w0, w1, e1 = ("e", 0, 0), ("w", 0, 0), ("w", 1, 0), ("e", 1, 0)
         x0, x1, f0, f1 = ("w", 0, 1), ("w", 1, 1), ("e", 0, 1), ("e", 1, 1)
-        load(*e0)
-        load(*w0)
-        load(*w1)
-        load(*e1)
-        for p in (x0, x1, f0, f1):
+        for p in (e0, w0, w1, e1, x0, x1, f0, f1):
             load(*p)
         warm_up("e", 0, 0, 4)
         warm_up("w", 0, 0, 4)
         warm_up("w", 1, 0, 2)
-        copy(*e0, 0, 1, "v")
-        copy(*e0, 1, 1, "s")
-        copy(*e0, 2, 1, "v")
-        copy(*e0, 3, 1, "s")
+        copy(*e0, 0, 2, "v")
+        copy(*e0, 2, 2, "s")
         quant(*e0, 0, 2)
         copy(*w0, 0, 2, "v")
         copy(*w0, 2, 2, "s")
         quant(*e0, 2, 2)
+        quant(*w0, 0, 2)
         copy(*w1, 0, 2, "v")
         copy(*w1, 2, 2, "s")
-        quant(*w0, 0, 4)
+        quant(*w0, 2, 2)
+        quant(*w1, 0, 2)
         copy(*e1, 0, 1, "v")
         copy(*e1, 1, 1, "s")
-        quant(*w1, 0, 4)
         quant(*e1, 0, 1)
-        quant(*e1, 1, 1)
-        copy(*e1, 2, 1, "v")
-        copy(*e1, 3, 1, "s")
+        quant(*w1, 2, 2)
         cells(0, 0)
+        copy(*e1, 3, 1, "s")
+        quant(*e1, 1, 1)
         cells(0, 1)
+        copy(*e1, 2, 1, "v")
         copy(*x0, 0, 2, "v")
         quant(*e1, 2, 2)
-        copy(*x0, 2, 2, "s")
         cells(0, 2)
         cells(0, 3)
+        copy(*x0, 2, 2, "s")
         copy(*x1, 0, 2, "v")
-        copy(*x1, 2, 2, "s")
-        quant(*x0, 0, 4)
+        quant(*x0, 0, 2)
         quant(*x1, 0, 2)
+        copy(*x1, 2, 2, "s")
+        for b in range(4):
+            cells(1, b, (0, 1))
+        quant(*x0, 2, 2)
         quant(*x1, 2, 2)
         for b in range(4):
-            copy_t(0, b)
-        for b in range(4):
-            cells(1, b)
+            cells(1, b, (2, 3))
         copy(*f0, 0, 2, "v")
         copy(*f1, 0, 2, "v")
-        for b in range(4):
-            copy_t(1, b)
+        for g2 in range(G):
+            for b in range(4):
+                copy_t(g2, b)
         quant(*f0, 0, 2)
         quant(*f1, 0, 2)
         quant_t(0)
@@ -212,9 +210,9 @@ def tile_parallelcoattention_kernel(tc, embedding, heatm, W_b, out):
         mm2(2, 0)
         mm2(3, 0)
         row_max(0, 0)
-        row_max(1, 0)
         quant(*f0, 2, 2)
         quant(*f1, 2, 2)
+        row_max(1, 0)
         row_max(2, 0)
         quant_t(4)
         row_max(3, 0)

@@ -54,18 +54,18 @@ def tile_parallelcoattention_kernel(tc, embedding, heatm, W_b, out):
         for kind in ("e", "w"):
             for h in range(2):
                 key = (kind, h)
-                grp[key] = keep.tile([P, G, HCOL, PACK], BF16, name="grp_%s%d" % key, align_bytes=64)
-                cod[key] = keep.tile([P, G, HCOL], U32, name="cod_%s%d" % key, align_bytes=64)
-                scl[key] = keep.tile([P, G, HCOL], U8, name="scl_%s%d" % key, align_bytes=64)
+                grp[key] = keep.tile([P, G, HCOL, PACK], BF16, name="grp_%s%d" % key, align_bytes=256)
+                cod[key] = keep.tile([P, G, HCOL], U32, name="cod_%s%d" % key, align_bytes=256)
+                scl[key] = keep.tile([P, G, HCOL], U8, name="scl_%s%d" % key, align_bytes=256)
                 for g in range(G):
                     raw[(kind, g, h)] = keep.tile([P, PACK, HCOL], BF16, name="raw_%s%d%d" % (kind, g, h))
         tgr = {}
         tcod = {}
         tscl = {}
         for b in range(NB):
-            tgr[b] = keep.tile([P, G, P, PACK], BF16, name="tgr%d" % b, align_bytes=64)
-            tcod[b] = keep.tile([P, G, P], U32, name="tcod%d" % b, align_bytes=64)
-            tscl[b] = keep.tile([P, G, P], U8, name="tscl%d" % b, align_bytes=64)
+            tgr[b] = keep.tile([P, G, P, PACK], BF16, name="tgr%d" % b, align_bytes=256)
+            tcod[b] = keep.tile([P, G, P], U32, name="tcod%d" % b, align_bytes=256)
+            tscl[b] = keep.tile([P, G, P], U8, name="tscl%d" % b, align_bytes=256)
         pts = {}
         pcs = {}
 

@@ -115,19 +115,19 @@ def tile_parallelcoattention_kernel(tc, embedding, heatm, W_b, out):
         def copy_t(g2, b):
             nc.scalar.copy(out=tgr[b][:, g2], in_=pts[(g2, b)][:].rearrange("p j n -> p n j"))
 
-        def quant_t(b):
+        def quant_t(b, g0=0, g1=G):
             nc.vector.quantize_mx(
-                out=tcod[b][:].rearrange("p g n -> p (g n)").bitcast(FP8X4),
-                scales=tscl[b][:].rearrange("p g n -> p (g n)"),
-                in_=tgr[b][:].rearrange("p g n t -> p (g n t)"),
+                out=tcod[b][:, g0:g1].rearrange("p g n -> p (g n)").bitcast(FP8X4),
+                scales=tscl[b][:, g0:g1].rearrange("p g n -> p (g n)"),
+                in_=tgr[b][:, g0:g1].rearrange("p g n t -> p (g n t)"),
             )
 
-        def mm2(b, h):
-            pc = psum.tile([P, HCOL], F32, name="pc", tag="bank")
-            pcs[(b, h)] = pc
-            for g2 in range(G):
+        def mm2(b, h, passes=range(G)):
+            if (b, h) not in pcs:
+                pcs[(b, h)] = psum.tile([P, HCOL], F32, name="pc", tag="bank")
+            for g2 in passes:
                 nc.tensor.matmul_mx(
-                    out=pc[:],
+                    out=pcs[(b, h)][:],
                     lhsT=tcod[b][:, g2, :].bitcast(FP8X4),
                     lhsT_scale=tscl[b][:, g2, :],
                     rhs=cod[("e", h)][:, g2, :].bitcast(FP8X4),
@@ -222,15 +222,21 @@ def tile_parallelcoattention_kernel(tc, embedding, heatm, W_b, out):
             mm2(b - 5, 1)
             cells(1, b)
             copy_t(1, b)
+            if b == 7:
+                quant_t(7, 0, 1)
             row_max(b - 5, 1)
             mm2(b - 1, 0)
             mm2(b - 1, 1)
             row_max(b - 1, 0)
-            quant_t(b)
+            if b == 7:
+                quant_t(7, 1, 2)
+            else:
+                quant_t(b)
             row_max(b - 1, 1)
         mm2(3, 1)
+        mm2(7, 0, (0,))
         row_max(3, 1)
-        mm2(7, 0)
+        mm2(7, 0, (1,))
         mm2(7, 1)
         row_max(7, 0)
         m8 = keep.tile([P, NB], F32, name="m8")

@@ -145,37 +145,33 @@ def tile_parallelcoattention_kernel(tc, embedding, heatm, W_b, out):
                 nc.tensor.matmul(out=junk[:], lhsT=raw[(kind, g, h)][:, 0, 0:P], rhs=raw[(kind, g, h)][:, 1, :],
                                  start=True, stop=True)
 
-        e0, w0, w1, e1 = ("e", 0, 0), ("w", 0, 0), ("w", 1, 0), ("e", 1, 0)
+        e0, e1, w0, w1 = ("e", 0, 0), ("e", 1, 0), ("w", 0, 0), ("w", 1, 0)
         x0, x1, f0, f1 = ("w", 0, 1), ("w", 1, 1), ("e", 0, 1), ("e", 1, 1)
-        for p in (e0, w0, w1, e1, x0, x1, f0, f1):
+        for p in (e0, e1, w0, w1, x0, x1, f0, f1):
             load(*p)
         warm_up("e", 0, 0, 4)
-        warm_up("w", 0, 0, 4)
-        warm_up("w", 1, 0, 2)
+        warm_up("e", 1, 0, 4)
+        warm_up("w", 0, 0, 2)
         copy(*e0, 0, 2, "v")
         copy(*e0, 2, 2, "s")
         quant(*e0, 0, 2)
+        copy(*e1, 0, 2, "v")
+        copy(*e1, 2, 2, "s")
+        quant(*e0, 2, 2)
+        quant(*e1, 0, 2)
         copy(*w0, 0, 2, "v")
         copy(*w0, 2, 2, "s")
-        quant(*e0, 2, 2)
-        quant(*w0, 0, 2)
+        quant(*e1, 2, 2)
         copy(*w1, 0, 2, "v")
         copy(*w1, 2, 2, "s")
-        quant(*w0, 2, 2)
+        quant(*w0, 0, 4)
         quant(*w1, 0, 2)
-        copy(*e1, 0, 1, "v")
-        copy(*e1, 1, 1, "s")
-        quant(*e1, 0, 1)
+        for b in range(4):
+            cells(0, b, (0, 1))
         quant(*w1, 2, 2)
-        cells(0, 0)
-        copy(*e1, 3, 1, "s")
-        quant(*e1, 1, 1)
-        cells(0, 1)
-        copy(*e1, 2, 1, "v")
+        for b in range(4):
+            cells(0, b, (2, 3))
         copy(*x0, 0, 2, "v")
-        quant(*e1, 2, 2)
-        cells(0, 2)
-        cells(0, 3)
         copy(*x0, 2, 2, "s")
         copy(*x1, 0, 2, "v")
         quant(*x0, 0, 2)
@@ -238,6 +234,7 @@ def tile_parallelcoattention_kernel(tc, embedding, heatm, W_b, out):
         row_max(3, 1)
         mm2(7, 0, (1,))
         mm2(7, 1)
+        warm_up("e", 0, 0, 4)
         row_max(7, 0)
         m8 = keep.tile([P, NB], F32, name="m8")
         nc.vector.reduce_max(out=m8[:, 0:NB - 1], in_=mx16[:, 0:2 * NB - 2].rearrange("p (b h) -> p b h", h=2), axis=AX.X)

@@ -152,6 +152,7 @@ def tile_parallelcoattention_kernel(tc, embedding, heatm, W_b, out):
         warm_up("e", 0, 0, 4)
         warm_up("e", 1, 0, 4)
         warm_up("w", 0, 0, 2)
+        warm_up("w", 1, 0, 3)
         copy(*e0, 0, 2, "v")
         copy(*e0, 2, 2, "s")
         quant(*e0, 0, 2)

@@ -65,7 +65,7 @@ def tile_parallelcoattention_kernel(tc, embedding, heatm, W_b, out):
         for b in range(NB):
             tgr[b] = keep.tile([P, G, P, PACK], BF16, name="tgr%d" % b, align_bytes=256)
             tcod[b] = keep.tile([P, G, P], U32, name="tcod%d" % b, align_bytes=256)
-            tscl[b] = keep.tile([P, G, P], U8, name="tscl%d" % b, align_bytes=256)
+            tscl[b] = keep.tile([P, G, 2 * P], U8, name="tscl%d" % b, align_bytes=256)
         pts = {}
         pcs = {}
 
@@ -115,12 +115,13 @@ def tile_parallelcoattention_kernel(tc, embedding, heatm, W_b, out):
         def copy_t(g2, b):
             nc.scalar.copy(out=tgr[b][:, g2], in_=pts[(g2, b)][:].rearrange("p j n -> p n j"))
 
-        def quant_t(b, g0=0, g1=G):
-            nc.vector.quantize_mx(
-                out=tcod[b][:, g0:g1].rearrange("p g n -> p (g n)").bitcast(FP8X4),
-                scales=tscl[b][:, g0:g1].rearrange("p g n -> p (g n)"),
-                in_=tgr[b][:, g0:g1].rearrange("p g n t -> p (g n t)"),
-            )
+        def quant_t(b, passes=range(G)):
+            for g2 in passes:
+                nc.vector.quantize_mx(
+                    out=tcod[b][:, g2].bitcast(FP8X4),
+                    scales=tscl[b][:, g2, 0:P],
+                    in_=tgr[b][:, g2].rearrange("p n t -> p (n t)"),
+                )
 
         def mm2(b, h, passes=range(G)):
             if (b, h) not in pcs:
@@ -129,7 +130,7 @@ def tile_parallelcoattention_kernel(tc, embedding, heatm, W_b, out):
                 nc.tensor.matmul_mx(
                     out=pcs[(b, h)][:],
                     lhsT=tcod[b][:, g2, :].bitcast(FP8X4),
-                    lhsT_scale=tscl[b][:, g2, :],
+                    lhsT_scale=tscl[b][:, g2, 0:P],
                     rhs=cod[("e", h)][:, g2, :].bitcast(FP8X4),
                     rhs_scale=scl[("e", h)][:, g2, :],
                     start=(g2 == 0),
@@ -219,16 +220,12 @@ def tile_parallelcoattention_kernel(tc, embedding, heatm, W_b, out):
             mm2(b - 5, 1)
             cells(1, b)
             copy_t(1, b)
-            if b == 7:
-                quant_t(7, 0, 1)
+            quant_t(b, (0,))
             row_max(b - 5, 1)
             mm2(b - 1, 0)
             mm2(b - 1, 1)
             row_max(b - 1, 0)
-            if b == 7:
-                quant_t(7, 1, 2)
-            else:
-                quant_t(b)
+            quant_t(b, (1,))
             row_max(b - 1, 1)
         mm2(3, 1)
         mm2(7, 0, (0,))

from contextlib import ExitStack

import concourse.mybir as mybir
from concourse.masks import make_identity

FLOPS = 2 * 2 * 1024 * 1024 * 1024
BYTES = 2 * 1024 * 1024 * 2 + 1024 * 4

F32 = mybir.dt.float32
BF16 = mybir.dt.bfloat16
U32 = mybir.dt.uint32
U8 = mybir.dt.uint8
FP8X4 = mybir.dt.float8_e4m3fn_x4
ACT = mybir.ActivationFunctionType
ALU = mybir.AluOpType
AX = mybir.AxisListType

P = 128
PACK = 4
G = 2
HCOL = 512
NB = 8


def tile_parallelcoattention_kernel(tc, embedding, heatm, W_b, out):
    nc = tc.nc
    e_rows = embedding[0].rearrange("(g p t) n -> p g t n", p=P, t=PACK)
    w_rows = W_b.rearrange("(g p t) n -> p g t n", p=P, t=PACK)
    out_rows = out[0].rearrange("(c q) u -> c (q u)", c=NB)

    with ExitStack() as ctx:
        keep = ctx.enter_context(tc.tile_pool(name="keep", bufs=1))
        psum = ctx.enter_context(tc.psum_pool(name="psum", bufs=8))
        ctx.enter_context(tc.manual_schedule())

        warm = keep.tile([P, 1], F32, name="warm")
        nc.vector.memset(warm[:], 0.0)
        warm2 = keep.tile([P, 1], F32, name="warm2")
        nc.scalar.activation(out=warm2[:], in_=warm[:], func=ACT.Tanh)
        ident = keep.tile([P, P], F32, name="ident")
        make_identity(nc, ident[:])
        ones = keep.tile([P, P], F32, name="ones")
        nc.vector.memset(ones[:], 1.0)
        epad = keep.tile([P, P], F32, name="epad")
        nc.vector.memset(epad[:], 0.0)
        shift = keep.tile([P, 1], F32, name="shift")
        nc.vector.memset(shift[:], -1.0)
        mx16 = keep.tile([P, 2 * NB], F32, name="mx16")

        raw = {}
        grp = {}
        cod = {}
        scl = {}
        for kind in ("e", "w"):
            for h in range(2):
                key = (kind, h)
                grp[key] = keep.tile([P, G, HCOL, PACK], BF16, name="grp_%s%d" % key, align_bytes=256)
                cod[key] = keep.tile([P, G, HCOL], U32, name="cod_%s%d" % key, align_bytes=256)
                scl[key] = keep.tile([P, G, HCOL], U8, name="scl_%s%d" % key, align_bytes=256)
                for g in range(G):
                    raw[(kind, g, h)] = keep.tile([P, PACK, HCOL], BF16, name="raw_%s%d%d" % (kind, g, h))
        tgr = {}
        tcod = {}
        tscl = {}
        for b in range(NB):
            tgr[b] = keep.tile([P, G, P, PACK], BF16, name="tgr%d" % b, align_bytes=256)
            tcod[b] = keep.tile([P, G, P], U32, name="tcod%d" % b, align_bytes=256)
            tscl[b] = keep.tile([P, G, 2 * P], U8, name="tscl%d" % b, align_bytes=256)
        pts = {}
        pcs = {}

        def cols(c0, n):
            return slice(c0 * P, (c0 + n) * P)

        def load(kind, g, h, c0=0, n=4):
            rows = e_rows if kind == "e" else w_rows
            nc.sync.dma_start(out=raw[(kind, g, h)][:, :, cols(c0, n)],
                              in_=rows[:, g, :, h * HCOL + c0 * P:h * HCOL + (c0 + n) * P])

        def copy(kind, g, h, c0, n, eng):
            if kind == "e":
                src = raw[(kind, g, h)][:, :, cols(c0, n)].rearrange("p t (c i) -> p c t i", i=4)
                dst = grp[(kind, h)][:, g, cols(c0, n), :].rearrange("p (c i) t -> p c t i", i=4)
            else:
                src = raw[(kind, g, h)][:].rearrange("p t (m u j) -> p j m t u", u=2, j=4)[:, c0:c0 + n]
                dst = grp[(kind, h)][:, g, cols(c0, n), :].rearrange("p (j m u) t -> p j m t u", u=2, m=P // 2)
            if eng == "v":
                nc.vector.tensor_copy(out=dst, in_=src)
            else:
                nc.scalar.copy(out=dst, in_=src)

        def quant(kind, g, h, c0, n):
            key = (kind, h)
            nc.vector.quantize_mx(
                out=cod[key][:, g, cols(c0, n)].bitcast(FP8X4),
                scales=scl[key][:, g, cols(c0, n)],
                in_=grp[key][:, g, cols(c0, n), :].rearrange("p n t -> p (n t)"),
            )

        def cells(g2, b, js=range(4)):
            if (g2, b) not in pts:
                pts[(g2, b)] = psum.tile([P, PACK, P], F32, name="pt", tag="bank")
            for j in js:
                for g1 in range(G):
                    nc.tensor.matmul_mx(
                        out=pts[(g2, b)][:, j, :],
                        lhsT=cod[("w", g2)][:, g1, cols(j, 1)].bitcast(FP8X4),
                        lhsT_scale=scl[("w", g2)][:, g1, cols(j, 1)],
                        rhs=cod[("e", b // 4)][:, g1, cols(b % 4, 1)].bitcast(FP8X4),
                        rhs_scale=scl[("e", b // 4)][:, g1, cols(b % 4, 1)],
                        start=(g1 == 0),
                        stop=(g1 == G - 1),
                    )

        def copy_t(g2, b):
            nc.scalar.copy(out=tgr[b][:, g2], in_=pts[(g2, b)][:].rearrange("p j n -> p n j"))

        def quant_t(b, passes=range(G)):
            for g2 in passes:
                nc.vector.quantize_mx(
                    out=tcod[b][:, g2].bitcast(FP8X4),
                    scales=tscl[b][:, g2, 0:P],
                    in_=tgr[b][:, g2].rearrange("p n t -> p (n t)"),
                )

        def mm2(b, h, passes=range(G)):
            if (b, h) not in pcs:
                pcs[(b, h)] = psum.tile([P, HCOL], F32, name="pc", tag="bank")
            for g2 in passes:
                nc.tensor.matmul_mx(
                    out=pcs[(b, h)][:],
                    lhsT=tcod[b][:, g2, :].bitcast(FP8X4),
                    lhsT_scale=tscl[b][:, g2, 0:P],
                    rhs=cod[("e", h)][:, g2, :].bitcast(FP8X4),
                    rhs_scale=scl[("e", h)][:, g2, :],
                    start=(g2 == 0),
                    stop=(g2 == G - 1),
                )

        def row_max(b, h):
            nc.vector.reduce_max(out=mx16[:, 2 * b + h:2 * b + h + 1], in_=pcs[(b, h)][:], axis=AX.X)

        def warm_up(kind, g, h, count):
            junk = psum.tile([P, HCOL], F32, name="junk", tag="bank")
            for i in range(count):
                nc.tensor.matmul(out=junk[:], lhsT=raw[(kind, g, h)][:, 0, 0:P], rhs=raw[(kind, g, h)][:, 1, :],
                                 start=True, stop=True)

        e0, e1, w0, w1 = ("e", 0, 0), ("e", 1, 0), ("w", 0, 0), ("w", 1, 0)
        x0, x1, f0, f1 = ("w", 0, 1), ("w", 1, 1), ("e", 0, 1), ("e", 1, 1)
        for p in (e0, e1, w0, w1, x0, x1, f0, f1):
            load(*p)
        warm_up("e", 0, 0, 4)
        warm_up("e", 1, 0, 4)
        warm_up("w", 0, 0, 2)
        warm_up("w", 1, 0, 3)
        copy(*e0, 0, 2, "v")
        copy(*e0, 2, 2, "s")
        quant(*e0, 0, 2)
        copy(*e1, 0, 2, "v")
        copy(*e1, 2, 2, "s")
        quant(*e0, 2, 2)
        quant(*e1, 0, 2)
        copy(*w0, 0, 2, "v")
        copy(*w0, 2, 2, "s")
        quant(*e1, 2, 2)
        copy(*w1, 0, 2, "v")
        copy(*w1, 2, 2, "s")
        quant(*w0, 0, 4)
        quant(*w1, 0, 2)
        for b in range(4):
            cells(0, b, (0, 1))
        quant(*w1, 2, 2)
        for b in range(4):
            cells(0, b, (2, 3))
        copy(*x0, 0, 2, "v")
        copy(*x0, 2, 2, "s")
        copy(*x1, 0, 2, "v")
        quant(*x0, 0, 2)
        quant(*x1, 0, 2)
        copy(*x1, 2, 2, "s")
        for b in range(4):
            cells(1, b, (0, 1))
        quant(*x0, 2, 2)
        quant(*x1, 2, 2)
        for b in range(4):
            cells(1, b, (2, 3))
        copy(*f0, 0, 2, "v")
        copy(*f1, 0, 2, "v")
        for g2 in range(G):
            for b in range(4):
                copy_t(g2, b)
        quant(*f0, 0, 2)
        quant(*f1, 0, 2)
        quant_t(0)
        quant_t(1)
        cells(0, 4)
        cells(1, 4)
        mm2(0, 0)
        mm2(1, 0)
        for p in (f0, f1):
            copy(*p, 3, 1, "s")
            copy(*p, 2, 1, "v")
        copy_t(0, 4)
        copy_t(1, 4)
        quant_t(2)
        quant_t(3)
        mm2(2, 0)
        mm2(3, 0)
        row_max(0, 0)
        quant(*f0, 2, 2)
        quant(*f1, 2, 2)
        row_max(1, 0)
        row_max(2, 0)
        quant_t(4)
        row_max(3, 0)
        for b in range(5, NB):
            cells(0, b)
            copy_t(0, b)
            mm2(b - 5, 1)
            cells(1, b)
            copy_t(1, b)
            quant_t(b, (0,))
            row_max(b - 5, 1)
            mm2(b - 1, 0)
            mm2(b - 1, 1)
            row_max(b - 1, 0)
            quant_t(b, (1,))
            row_max(b - 1, 1)
        mm2(3, 1)
        mm2(7, 0, (0,))
        row_max(3, 1)
        mm2(7, 0, (1,))
        mm2(7, 1)
        warm_up("e", 0, 0, 4)
        row_max(7, 0)
        m8 = keep.tile([P, NB], F32, name="m8")
        nc.vector.reduce_max(out=m8[:, 0:NB - 1], in_=mx16[:, 0:2 * NB - 2].rearrange("p (b h) -> p b h", h=2), axis=AX.X)
        junk_max = keep.tile([P, HCOL], F32, name="junk_max")
        nc.vector.tensor_scalar(out=junk_max[:], in0=pcs[(7, 1)][:], scalar1=0.0, scalar2=mx16[:, 14:15], op0=ALU.add,
                                op1=ALU.max, accum_out=m8[:, NB - 1:NB])

        th = keep.tile([P, NB], F32, name="th")
        nc.scalar.activation(out=th[:], in_=m8[:], func=ACT.Tanh)
        rsum = keep.tile([P, 1], F32, name="rsum")
        nc.scalar.activation(out=epad[:, 0:NB], in_=th[:], func=ACT.Exp, bias=shift[:, 0:1], scale=1.0,
                             accum_out=rsum[:])
        tot = psum.tile([P, 1], F32, name="tot", tag="bank")
        nc.tensor.matmul(out=tot[:], lhsT=ones[:], rhs=rsum[:], start=True, stop=True)
        et = psum.tile([P, P], F32, name="et", tag="bank")
        nc.tensor.transpose(et[:], epad[:], ident[:])
        rc = keep.tile([P, 1], F32, name="rc")
        nc.vector.reciprocal(out=rc[:], in_=tot[:])
        res = keep.tile([P, P], F32, name="res")
        nc.vector.tensor_scalar(out=res[:], in0=et[:], scalar1=rc[:, 0:1], scalar2=None, op0=ALU.mult)
        nc.sync.dma_start(out=out_rows, in_=res[0:NB, :])
